import numpy as np
import ml_dtypes


def mxq(x, axis, fmt="e4m3"):
    dtype, down = {"e4m3": (ml_dtypes.float8_e4m3fn, 7), "e5m2": (ml_dtypes.float8_e5m2, 14)}[fmt]
    v = np.moveaxis(np.asarray(x, np.float32).astype(ml_dtypes.bfloat16).astype(np.float64), axis, -1)
    blocks = v.reshape(v.shape[:-1] + (-1, 32))
    amax = np.abs(blocks).max(-1, keepdims=True)
    byte = np.maximum(np.where(amax > 0, np.frexp(amax)[1] - 1 + 127, 0) - down, 1)
    scale = np.exp2(byte - 127.0)
    codes = (blocks / scale).astype(np.float32).astype(dtype).astype(np.float64)
    return np.moveaxis((codes * scale).reshape(v.shape), -1, axis)


WIDE = False


def mx_kscale(k):
    if not WIDE:
        return np.ones(k)
    levels = np.array([10, -10, 5, -5, 0])
    if k % 512:
        return np.exp2(np.random.permutation(np.resize(levels, k // 32))).repeat(32)
    a = np.empty((k // 512, 16))
    for p in range(k // 512):
        a[p, :8] = np.random.permutation(np.resize(levels, 8))
        for g in range(8):
            far = levels[np.abs(levels - a[p, g]) >= 10]
            a[p, g + 8] = far[np.random.randint(len(far))]
    return np.exp2(a.ravel()).repeat(32)


BF16 = ml_dtypes.bfloat16


def bf(x):
    return np.asarray(x, np.float32).astype(BF16)


def f64(x):
    return np.asarray(x).astype(np.float64)


N_A, N_P, D = 512, 8192, 512
TEMPERATURE = 0.07
SIG = 3.5
SA = np.sqrt(SIG * TEMPERATURE / np.sqrt(D))
SP = SA * np.sqrt(SIG ** 2 - 2.0 * np.log(N_P / N_A)) / SIG


def logsumexp(v):
    m = v.max(axis=1, keepdims=True)
    return m[:, 0] + np.log(np.exp(v - m).sum(axis=1))


def setup_inputs():
    s = mx_kscale(D)
    c = np.mean(s ** 4) ** -0.25
    return {"anchor": bf(np.random.standard_normal((N_A, D)) * SA * s * c),
            "pos": bf(np.random.standard_normal((N_P, D)) * SP / (s * c))}


def reference(anchor, pos):
    aq = mxq(f64(anchor), 1, "e4m3")
    sim_pos = (aq @ mxq(f64(pos), 1, "e4m3").T) / TEMPERATURE
    sim_neg = (aq @ aq.T) / TEMPERATURE
    sim_neg = np.where(np.eye(aq.shape[0], dtype=bool), -np.inf, sim_neg)
    numerator = logsumexp(sim_pos)
    denominator = np.logaddexp(numerator, logsumexp(sim_neg))
    return numerator - denominator

@@ -1,0 +1,201 @@
+from contextlib import ExitStack
+
+import concourse.mybir as mybir
+from concourse.masks import make_identity
+
+F32 = mybir.dt.float32
+BF16 = mybir.dt.bfloat16
+U32 = mybir.dt.uint32
+U8 = mybir.dt.uint8
+FP8X4 = mybir.dt.float8_e4m3fn_x4
+ALU = mybir.AluOpType
+ACT = mybir.ActivationFunctionType
+AXIS = mybir.AxisListType
+
+P = 128
+N_A, N_P, D = 512, 8192, 512
+TEMPERATURE = 0.07
+FLOPS = 2 * N_A * D * (N_P + N_A)
+
+PACK = 4
+WORDS = D // 2
+A_TILES = N_A // P
+PASS_COLS = 512
+LOAD_ROWS = 512
+PASSES = 2
+LAST = PASSES - 1
+BLOCK = PASSES * PASS_COLS
+N_BLOCKS = N_P // BLOCK
+BLOCK_ROW_TILES = BLOCK // P
+AHEAD = 2
+N_STATS = N_BLOCKS + 1
+NEGATIVES = N_BLOCKS
+BANK_ROW_TILES = 2
+VECTOR_EVERY = 4
+MASKED = 1.0e38
+
+
+def transpose_rows(nc, psum_words, identity, raw_words, grouped_words):
+    for bank in range(raw_words.shape[1] // BANK_ROW_TILES):
+        flipped = psum_words.tile([P, 2, BANK_ROW_TILES * P], F32, name="flipped")
+        for half in range(2):
+            for i in range(BANK_ROW_TILES):
+                nc.tensor.transpose(
+                    flipped[:, half, i * P : (i + 1) * P],
+                    raw_words[:, bank * BANK_ROW_TILES + i, half:WORDS:2],
+                    identity[:],
+                )
+        rows = slice(bank * BANK_ROW_TILES * P, (bank + 1) * BANK_ROW_TILES * P)
+        if bank % VECTOR_EVERY == VECTOR_EVERY - 1:
+            nc.vector.tensor_copy(out=grouped_words[:, rows, :], in_=flipped[:].rearrange("p u c -> p c u"))
+        else:
+            nc.scalar.copy(out=grouped_words[:, rows, :], in_=flipped[:].rearrange("p u c -> p c u"))
+
+
+def tile_crossgenderinfonceloss_pa_t_kernel(tc, anchor, pos, out):
+    nc = tc.nc
+    with ExitStack() as ctx:
+        keep = ctx.enter_context(tc.tile_pool(name="keep", bufs=1))
+        stage = ctx.enter_context(tc.tile_pool(name="stage", bufs=3))
+        psum_words = ctx.enter_context(tc.psum_pool(name="psum_words", bufs=4))
+        psum_scores = ctx.enter_context(tc.psum_pool(name="psum_scores", bufs=4))
+
+        a_raw = keep.tile([P, A_TILES * D], BF16)
+        nc.sync.dma_start(
+            out=a_raw[:].rearrange("p (t k) -> p t k", t=A_TILES),
+            in_=anchor.rearrange("(t p) k -> p t k", p=P),
+        )
+        p_raw = keep.tile([P, (N_P // P) * D], BF16)
+        load_cols = (LOAD_ROWS // P) * D
+        pos_loads = pos.rearrange("(c p r) k -> c p (r k)", p=P, r=LOAD_ROWS // P)
+        for c in range(N_P // LOAD_ROWS):
+            nc.sync.dma_start(out=p_raw[:, c * load_cols : (c + 1) * load_cols], in_=pos_loads[c])
+        a_raw_words = a_raw[:].bitcast(F32).rearrange("p (r w) -> p r w", w=WORDS)
+        p_raw_words = p_raw[:].bitcast(F32).rearrange("p (r w) -> p r w", w=WORDS)
+
+        identity = keep.tile([P, P], F32)
+        make_identity(nc, identity[:])
+        result = keep.tile([P, P], F32)
+        nc.vector.memset(result[:], 0.0)
+
+        a_codes = keep.tile([P, N_A], U32, align_bytes=64)
+        a_scales = keep.tile([P, N_A], U8, align_bytes=64)
+        p_codes = keep.tile([P, N_P], U32, align_bytes=64)
+        p_scales = keep.tile([P, N_P], U8, align_bytes=64)
+        lowest = keep.tile([P, A_TILES, N_STATS, PASSES], F32)
+        sums = keep.tile([P, A_TILES, N_STATS], F32)
+
+        def transpose_block(b):
+            grouped = stage.tile([P, BLOCK * PACK], BF16, name="grouped", bufs=AHEAD, align_bytes=64)
+            transpose_rows(
+                nc, psum_words, identity,
+                p_raw_words[:, b * BLOCK_ROW_TILES : (b + 1) * BLOCK_ROW_TILES, :],
+                grouped[:].bitcast(F32).rearrange("p (c u) -> p c u", u=2),
+            )
+            return grouped
+
+        def quantise_block(b, grouped):
+            nc.vector.quantize_mx(
+                out=p_codes[:, b * BLOCK : (b + 1) * BLOCK].bitcast(FP8X4),
+                scales=p_scales[:, b * BLOCK : (b + 1) * BLOCK],
+                in_=grouped[:],
+            )
+
+        def scores(t, moving_codes, moving_scales):
+            acc = psum_scores.tile([P, PASS_COLS], F32, name="acc")
+            nc.tensor.matmul_mx(
+                out=acc[:],
+                lhsT=a_codes[:, t * P : (t + 1) * P].bitcast(FP8X4),
+                lhsT_scale=a_scales[:, t * P : (t + 1) * P],
+                rhs=moving_codes.bitcast(FP8X4),
+                rhs_scale=moving_scales,
+                start=True,
+                stop=True,
+            )
+            return acc
+
+        def score_pair(b, x, first):
+            for h in range(PASSES):
+                cols = slice(b * BLOCK + h * PASS_COLS, b * BLOCK + (h + 1) * PASS_COLS)
+                for t in (first, first + 1):
+                    acc = scores(t, p_codes[:, cols], p_scales[:, cols])
+                    nc.vector.tensor_scalar(
+                        out=x[t][:, h * PASS_COLS : (h + 1) * PASS_COLS], in0=acc[:],
+                        scalar1=-1.0 / TEMPERATURE,
+                        scalar2=None if h == 0 else lowest[:, t, b, h - 1 : h],
+                        op0=ALU.mult, op1=ALU.min,
+                        accum_out=lowest[:, t, b, h : h + 1],
+                    )
+
+        def score_negatives():
+            x = [stage.tile([P, N_A], F32, name="x_neg%d" % t, bufs=1) for t in range(A_TILES)]
+            for t in range(A_TILES):
+                acc = scores(t, a_codes[:], a_scales[:])
+                nc.scalar.mul(out=x[t][:], in_=acc[:], mul=-1.0 / TEMPERATURE)
+                own = x[t][:, t * P : (t + 1) * P]
+                nc.gpsimd.affine_select(
+                    out=own, in_=own, pattern=[[-1, P]], compare_op=ALU.not_equal,
+                    fill=MASKED, base=0, channel_multiplier=1,
+                )
+                nc.vector.tensor_reduce(
+                    out=lowest[:, t, NEGATIVES, LAST : LAST + 1], in_=x[t][:], axis=AXIS.X, op=ALU.min
+                )
+            return x
+
+        def exponentials(s, x):
+            for t in range(A_TILES):
+                nc.scalar.activation(
+                    out=x[t][:], in_=x[t][:], func=ACT.Exp,
+                    bias=lowest[:, t, s, LAST : LAST + 1], scale=-1.0,
+                    accum_out=sums[:, t, s : s + 1],
+                )
+
+        a_grouped = keep.tile([P, N_A * PACK], BF16, align_bytes=64)
+        transpose_rows(
+            nc, psum_words, identity, a_raw_words,
+            a_grouped[:].bitcast(F32).rearrange("p (c u) -> p c u", u=2),
+        )
+        nc.vector.quantize_mx(out=a_codes[:].bitcast(FP8X4), scales=a_scales[:], in_=a_grouped[:])
+        grouped = {0: transpose_block(0)}
+        quantise_block(0, grouped[0])
+        x_negatives = score_negatives()
+        for b in range(1, AHEAD):
+            grouped[b] = transpose_block(b)
+        exponentials(NEGATIVES, x_negatives)
+
+        for b in range(N_BLOCKS):
+            if b + 1 < N_BLOCKS:
+                quantise_block(b + 1, grouped[b + 1])
+            x = [stage.tile([P, BLOCK], F32, name="x%d" % t) for t in range(A_TILES)]
+            score_pair(b, x, 0)
+            if b + AHEAD < N_BLOCKS:
+                grouped[b + AHEAD] = transpose_block(b + AHEAD)
+            score_pair(b, x, 2)
+            exponentials(b, x)
+
+        ALL, POSITIVES = 0, 1
+        low = keep.tile([P, A_TILES, 2], F32)
+        nc.vector.tensor_reduce(out=low[:, :, ALL], in_=lowest[:, :, :, LAST], axis=AXIS.X, op=ALU.min)
+        nc.vector.tensor_reduce(
+            out=low[:, :, POSITIVES], in_=lowest[:, :, 0:N_BLOCKS, LAST], axis=AXIS.X, op=ALU.min
+        )
+        both = [P, A_TILES, 2, N_STATS]
+        weight = keep.tile(both, F32)
+        nc.vector.tensor_tensor(
+            out=weight[:], in0=low[:].unsqueeze(3).to_broadcast(both),
+            in1=lowest[:, :, :, LAST].unsqueeze(2).to_broadcast(both), op=ALU.subtract,
+        )
+        nc.vector.memset(weight[:, :, POSITIVES, NEGATIVES], -MASKED)
+        nc.scalar.activation(out=weight[:], in_=weight[:], func=ACT.Exp)
+        nc.vector.tensor_mul(out=weight[:], in0=weight[:], in1=sums[:].unsqueeze(2).to_broadcast(both))
+        lse = keep.tile([P, A_TILES, 2], F32)
+        nc.vector.tensor_reduce(out=lse[:], in_=weight[:], axis=AXIS.X, op=ALU.add)
+        nc.scalar.activation(out=lse[:], in_=lse[:], func=ACT.Ln)
+        nc.vector.tensor_sub(out=lse[:], in0=lse[:], in1=low[:])
+        nc.vector.tensor_sub(out=result[:, 0:A_TILES], in0=lse[:, :, POSITIVES], in1=lse[:, :, ALL])
+
+        result_rows_psum = psum_words.tile([P, P], F32, name="flipped")
+        nc.tensor.transpose(result_rows_psum[:], result[:], identity[:])
+        result_rows = keep.tile([P, P], F32)
+        nc.vector.tensor_copy(out=result_rows[:], in_=result_rows_psum[:])
+        nc.sync.dma_start(out=out.rearrange("(t p) -> t p", p=P), in_=result_rows[0:A_TILES, :])

@@ -20,36 +20,14 @@ FLOPS = 2 * N_A * D * (N_P + N_A)
 PACK = 4
 WORDS = D // 2
 A_TILES = N_A // P
-PASS_COLS = 512
-LOAD_ROWS = 512
-PASSES = 2
-LAST = PASSES - 1
-BLOCK = PASSES * PASS_COLS
+BLOCK = 512
 N_BLOCKS = N_P // BLOCK
-BLOCK_ROW_TILES = BLOCK // P
-AHEAD = 2
+ROW_TILES = BLOCK // P
 N_STATS = N_BLOCKS + 1
 NEGATIVES = N_BLOCKS
-BANK_ROW_TILES = 2
-VECTOR_EVERY = 4
-MASKED = 1.0e38
-
-
-def transpose_rows(nc, psum_words, identity, raw_words, grouped_words):
-    for bank in range(raw_words.shape[1] // BANK_ROW_TILES):
-        flipped = psum_words.tile([P, 2, BANK_ROW_TILES * P], F32, name="flipped")
-        for half in range(2):
-            for i in range(BANK_ROW_TILES):
-                nc.tensor.transpose(
-                    flipped[:, half, i * P : (i + 1) * P],
-                    raw_words[:, bank * BANK_ROW_TILES + i, half:WORDS:2],
-                    identity[:],
-                )
-        rows = slice(bank * BANK_ROW_TILES * P, (bank + 1) * BANK_ROW_TILES * P)
-        if bank % VECTOR_EVERY == VECTOR_EVERY - 1:
-            nc.vector.tensor_copy(out=grouped_words[:, rows, :], in_=flipped[:].rearrange("p u c -> p c u"))
-        else:
-            nc.scalar.copy(out=grouped_words[:, rows, :], in_=flipped[:].rearrange("p u c -> p c u"))
+BANK_TILES = 2
+BANKS = ROW_TILES // BANK_TILES
+MASKED = -1.0e36
 
 
 def tile_crossgenderinfonceloss_pa_t_kernel(tc, anchor, pos, out):
@@ -57,8 +35,9 @@ def tile_crossgenderinfonceloss_pa_t_kernel(tc, anchor, pos, out):
     with ExitStack() as ctx:
         keep = ctx.enter_context(tc.tile_pool(name="keep", bufs=1))
         stage = ctx.enter_context(tc.tile_pool(name="stage", bufs=3))
-        psum_words = ctx.enter_context(tc.psum_pool(name="psum_words", bufs=4))
-        psum_scores = ctx.enter_context(tc.psum_pool(name="psum_scores", bufs=4))
+        psum_words = ctx.enter_context(tc.psum_pool(name="psum_words", bufs=3))
+        psum_scores = ctx.enter_context(tc.psum_pool(name="psum_scores", bufs=5))
+        ctx.enter_context(tc.manual_schedule())
 
         a_raw = keep.tile([P, A_TILES * D], BF16)
         nc.sync.dma_start(
@@ -66,15 +45,18 @@ def tile_crossgenderinfonceloss_pa_t_kernel(tc, anchor, pos, out):
             in_=anchor.rearrange("(t p) k -> p t k", p=P),
         )
         p_raw = keep.tile([P, (N_P // P) * D], BF16)
-        load_cols = (LOAD_ROWS // P) * D
-        pos_loads = pos.rearrange("(c p r) k -> c p (r k)", p=P, r=LOAD_ROWS // P)
-        for c in range(N_P // LOAD_ROWS):
+        load_cols = ROW_TILES * D
+        pos_loads = pos.rearrange("(c p r) k -> c p (r k)", p=P, r=ROW_TILES)
+        for c in range(N_BLOCKS):
             nc.sync.dma_start(out=p_raw[:, c * load_cols : (c + 1) * load_cols], in_=pos_loads[c])
         a_raw_words = a_raw[:].bitcast(F32).rearrange("p (r w) -> p r w", w=WORDS)
         p_raw_words = p_raw[:].bitcast(F32).rearrange("p (r w) -> p r w", w=WORDS)
 
         identity = keep.tile([P, P], F32)
         make_identity(nc, identity[:])
+        ones = keep.tile([P, 1], F32)
+        nc.vector.memset(ones[:], 1.0)
+        nc.scalar.activation(out=ones[:], in_=ones[:], func=ACT.Ln)
         result = keep.tile([P, P], F32)
         nc.vector.memset(result[:], 0.0)
 
@@ -82,27 +64,37 @@ def tile_crossgenderinfonceloss_pa_t_kernel(tc, anchor, pos, out):
         a_scales = keep.tile([P, N_A], U8, align_bytes=64)
         p_codes = keep.tile([P, N_P], U32, align_bytes=64)
         p_scales = keep.tile([P, N_P], U8, align_bytes=64)
-        lowest = keep.tile([P, A_TILES, N_STATS, PASSES], F32)
+        largest = keep.tile([P, N_STATS, A_TILES], F32)
+        lowest = keep.tile([P, A_TILES, N_STATS], F32)
         sums = keep.tile([P, A_TILES, N_STATS], F32)
 
-        def transpose_block(b):
-            grouped = stage.tile([P, BLOCK * PACK], BF16, name="grouped", bufs=AHEAD, align_bytes=64)
-            transpose_rows(
-                nc, psum_words, identity,
-                p_raw_words[:, b * BLOCK_ROW_TILES : (b + 1) * BLOCK_ROW_TILES, :],
-                grouped[:].bitcast(F32).rearrange("p (c u) -> p c u", u=2),
-            )
-            return grouped
+        def transposes(raw_words):
+            banks = []
+            for bank in range(BANKS):
+                flipped = psum_words.tile([P, 2, BANK_TILES * P], F32, name="flipped")
+                for u in range(2):
+                    for i in range(BANK_TILES):
+                        nc.tensor.transpose(
+                            flipped[:, u, i * P : (i + 1) * P],
+                            raw_words[:, bank * BANK_TILES + i, u:WORDS:2],
+                            identity[:],
+                        )
+                banks.append(flipped)
+            return banks
 
-        def quantise_block(b, grouped):
-            nc.vector.quantize_mx(
-                out=p_codes[:, b * BLOCK : (b + 1) * BLOCK].bitcast(FP8X4),
-                scales=p_scales[:, b * BLOCK : (b + 1) * BLOCK],
-                in_=grouped[:],
-            )
+        def new_grouped():
+            return stage.tile([P, BLOCK * PACK], BF16, name="grouped", align_bytes=64)
 
-        def scores(t, moving_codes, moving_scales):
-            acc = psum_scores.tile([P, PASS_COLS], F32, name="acc")
+        def empty_bank(copy, grouped, banks, bank):
+            words = grouped[:].bitcast(F32).rearrange("p (c u) -> p c u", u=2)
+            rows = slice(bank * BANK_TILES * P, (bank + 1) * BANK_TILES * P)
+            copy(out=words[:, rows, :], in_=banks[bank][:].rearrange("p u c -> p c u"))
+
+        def quantise(codes, scales, grouped):
+            nc.vector.quantize_mx(out=codes.bitcast(FP8X4), scales=scales, in_=grouped[:])
+
+        def score(t, moving_codes, moving_scales):
+            acc = psum_scores.tile([P, BLOCK], F32, name="acc")
             nc.tensor.matmul_mx(
                 out=acc[:],
                 lhsT=a_codes[:, t * P : (t + 1) * P].bitcast(FP8X4),
@@ -114,85 +106,101 @@ def tile_crossgenderinfonceloss_pa_t_kernel(tc, anchor, pos, out):
             )
             return acc
 
-        def score_pair(b, x, first):
-            for h in range(PASSES):
-                cols = slice(b * BLOCK + h * PASS_COLS, b * BLOCK + (h + 1) * PASS_COLS)
-                for t in (first, first + 1):
-                    acc = scores(t, p_codes[:, cols], p_scales[:, cols])
-                    nc.vector.tensor_scalar(
-                        out=x[t][:, h * PASS_COLS : (h + 1) * PASS_COLS], in0=acc[:],
-                        scalar1=-1.0 / TEMPERATURE,
-                        scalar2=None if h == 0 else lowest[:, t, b, h - 1 : h],
-                        op0=ALU.mult, op1=ALU.min,
-                        accum_out=lowest[:, t, b, h : h + 1],
-                    )
+        def find_largest(s, t, x):
+            nc.vector.tensor_reduce(out=largest[:, s, t : t + 1], in_=x[:], axis=AXIS.X, op=ALU.max)
 
-        def score_negatives():
-            x = [stage.tile([P, N_A], F32, name="x_neg%d" % t, bufs=1) for t in range(A_TILES)]
-            for t in range(A_TILES):
-                acc = scores(t, a_codes[:], a_scales[:])
-                nc.scalar.mul(out=x[t][:], in_=acc[:], mul=-1.0 / TEMPERATURE)
-                own = x[t][:, t * P : (t + 1) * P]
-                nc.gpsimd.affine_select(
-                    out=own, in_=own, pattern=[[-1, P]], compare_op=ALU.not_equal,
-                    fill=MASKED, base=0, channel_multiplier=1,
-                )
-                nc.vector.tensor_reduce(
-                    out=lowest[:, t, NEGATIVES, LAST : LAST + 1], in_=x[t][:], axis=AXIS.X, op=ALU.min
-                )
-            return x
+        def scale_largest(s, first, count):
+            tiles = slice(first, first + count)
+            nc.gpsimd.tensor_scalar(
+                out=lowest[:, tiles, s], in0=largest[:, s, tiles],
+                scalar1=-1.0 / TEMPERATURE, scalar2=0.0, op0=ALU.mult, op1=ALU.add,
+            )
 
-        def exponentials(s, x):
-            for t in range(A_TILES):
-                nc.scalar.activation(
-                    out=x[t][:], in_=x[t][:], func=ACT.Exp,
-                    bias=lowest[:, t, s, LAST : LAST + 1], scale=-1.0,
-                    accum_out=sums[:, t, s : s + 1],
-                )
+        def exponential(s, t, x):
+            weights = stage.tile([P, BLOCK], F32, name="weights")
+            nc.scalar.activation(
+                out=weights[:], in_=x[:], func=ACT.Exp,
+                bias=lowest[:, t, s : s + 1], scale=1.0 / TEMPERATURE,
+                accum_out=sums[:, t, s : s + 1],
+            )
 
-        a_grouped = keep.tile([P, N_A * PACK], BF16, align_bytes=64)
-        transpose_rows(
-            nc, psum_words, identity, a_raw_words,
-            a_grouped[:].bitcast(F32).rearrange("p (c u) -> p c u", u=2),
-        )
-        nc.vector.quantize_mx(out=a_codes[:].bitcast(FP8X4), scales=a_scales[:], in_=a_grouped[:])
-        grouped = {0: transpose_block(0)}
+        def block_words(b):
+            return p_raw_words[:, b * ROW_TILES : (b + 1) * ROW_TILES, :]
+
+        def quantise_block(b, grouped):
+            cols = slice(b * BLOCK, (b + 1) * BLOCK)
+            quantise(p_codes[:, cols], p_scales[:, cols], grouped)
+
+        a_banks = transposes(a_raw_words)
+        a_grouped = new_grouped()
+        empty_bank(nc.scalar.copy, a_grouped, a_banks, 0)
+        empty_bank(nc.vector.tensor_copy, a_grouped, a_banks, 1)
+        banks = transposes(block_words(0))
+        grouped = {0: new_grouped()}
+        empty_bank(nc.scalar.copy, grouped[0], banks, 0)
+        quantise(a_codes[:], a_scales[:], a_grouped)
+        empty_bank(nc.vector.tensor_copy, grouped[0], banks, 1)
         quantise_block(0, grouped[0])
-        x_negatives = score_negatives()
-        for b in range(1, AHEAD):
-            grouped[b] = transpose_block(b)
-        exponentials(NEGATIVES, x_negatives)
+
+        negatives = []
+        for t in range(A_TILES):
+            acc = score(t, a_codes[:], a_scales[:])
+            x = stage.tile([P, N_A], F32, name="x%d" % t, bufs=1)
+            nc.scalar.copy(out=x[:], in_=acc[:])
+            own = x[:, t * P : (t + 1) * P]
+            nc.gpsimd.affine_select(
+                out=own, in_=own, pattern=[[-1, P]], compare_op=ALU.not_equal,
+                fill=MASKED, base=0, channel_multiplier=1,
+            )
+            negatives.append(x)
+        banks = transposes(block_words(1))
+        grouped[1] = new_grouped()
+        empty_bank(nc.scalar.copy, grouped[1], banks, 0)
+        empty_bank(nc.vector.tensor_copy, grouped[1], banks, 1)
+        for t in range(A_TILES):
+            find_largest(NEGATIVES, t, negatives[t])
+        scale_largest(NEGATIVES, 0, A_TILES)
+        for t in range(A_TILES):
+            exponential(NEGATIVES, t, negatives[t])
 
         for b in range(N_BLOCKS):
-            if b + 1 < N_BLOCKS:
-                quantise_block(b + 1, grouped[b + 1])
-            x = [stage.tile([P, BLOCK], F32, name="x%d" % t) for t in range(A_TILES)]
-            score_pair(b, x, 0)
-            if b + AHEAD < N_BLOCKS:
-                grouped[b + AHEAD] = transpose_block(b + AHEAD)
-            score_pair(b, x, 2)
-            exponentials(b, x)
+            cols = slice(b * BLOCK, (b + 1) * BLOCK)
+            accs = [score(t, p_codes[:, cols], p_scales[:, cols]) for t in range(A_TILES)]
+            if b + 2 < N_BLOCKS:
+                banks = transposes(block_words(b + 2))
+                grouped[b + 2] = new_grouped()
+            for pair in range(2):
+                for t in (2 * pair, 2 * pair + 1):
+                    find_largest(b, t, accs[t])
+                scale_largest(b, 2 * pair, 2)
+                if pair == 0 and b + 1 < N_BLOCKS:
+                    quantise_block(b + 1, grouped[b + 1])
+                for t in (2 * pair, 2 * pair + 1):
+                    exponential(b, t, accs[t])
+                if b + 2 < N_BLOCKS:
+                    on_vector = pair == 1 and b % 2 == 1
+                    empty_bank(nc.vector.tensor_copy if on_vector else nc.scalar.copy, grouped[b + 2], banks, pair)
 
         ALL, POSITIVES = 0, 1
         low = keep.tile([P, A_TILES, 2], F32)
-        nc.vector.tensor_reduce(out=low[:, :, ALL], in_=lowest[:, :, :, LAST], axis=AXIS.X, op=ALU.min)
-        nc.vector.tensor_reduce(
-            out=low[:, :, POSITIVES], in_=lowest[:, :, 0:N_BLOCKS, LAST], axis=AXIS.X, op=ALU.min
-        )
+        nc.vector.tensor_reduce(out=low[:, :, ALL], in_=lowest[:], axis=AXIS.X, op=ALU.min)
+        nc.vector.tensor_reduce(out=low[:, :, POSITIVES], in_=lowest[:, :, 0:N_BLOCKS], axis=AXIS.X, op=ALU.min)
         both = [P, A_TILES, 2, N_STATS]
         weight = keep.tile(both, F32)
         nc.vector.tensor_tensor(
             out=weight[:], in0=low[:].unsqueeze(3).to_broadcast(both),
-            in1=lowest[:, :, :, LAST].unsqueeze(2).to_broadcast(both), op=ALU.subtract,
+            in1=lowest[:].unsqueeze(2).to_broadcast(both), op=ALU.subtract,
         )
-        nc.vector.memset(weight[:, :, POSITIVES, NEGATIVES], -MASKED)
+        nc.vector.memset(weight[:, :, POSITIVES, NEGATIVES], MASKED)
+        shift = keep.tile([P, A_TILES], F32)
+        nc.vector.tensor_sub(out=shift[:], in0=low[:, :, ALL], in1=low[:, :, POSITIVES])
         nc.scalar.activation(out=weight[:], in_=weight[:], func=ACT.Exp)
         nc.vector.tensor_mul(out=weight[:], in0=weight[:], in1=sums[:].unsqueeze(2).to_broadcast(both))
         lse = keep.tile([P, A_TILES, 2], F32)
         nc.vector.tensor_reduce(out=lse[:], in_=weight[:], axis=AXIS.X, op=ALU.add)
         nc.scalar.activation(out=lse[:], in_=lse[:], func=ACT.Ln)
-        nc.vector.tensor_sub(out=lse[:], in0=lse[:], in1=low[:])
-        nc.vector.tensor_sub(out=result[:, 0:A_TILES], in0=lse[:, :, POSITIVES], in1=lse[:, :, ALL])
+        nc.vector.tensor_sub(out=lse[:, :, POSITIVES], in0=lse[:, :, POSITIVES], in1=lse[:, :, ALL])
+        nc.vector.tensor_add(out=result[:, 0:A_TILES], in0=lse[:, :, POSITIVES], in1=shift[:])
 
         result_rows_psum = psum_words.tile([P, P], F32, name="flipped")
         nc.tensor.transpose(result_rows_psum[:], result[:], identity[:])

@@ -23,9 +23,10 @@ A_TILES = N_A // P
 BLOCK = 512
 N_BLOCKS = N_P // BLOCK
 ROW_TILES = BLOCK // P
-N_STATS = N_BLOCKS + 1
-NEGATIVES = N_BLOCKS
+OTHER_TILES, OWN_TILE, FIRST_BLOCK = 0, 1, 2
+N_STATS = FIRST_BLOCK + N_BLOCKS
 BANK_TILES = 2
+AHEAD = 3
 BANKS = ROW_TILES // BANK_TILES
 MASKED = -1.0e36
 
@@ -40,10 +41,12 @@ def tile_crossgenderinfonceloss_pa_t_kernel(tc, anchor, pos, out):
         ctx.enter_context(tc.manual_schedule())
 
         a_raw = keep.tile([P, A_TILES * D], BF16)
-        nc.sync.dma_start(
-            out=a_raw[:].rearrange("p (t k) -> p t k", t=A_TILES),
-            in_=anchor.rearrange("(t p) k -> p t k", p=P),
-        )
+        for bank in range(BANKS):
+            tiles = slice(bank * BANK_TILES, (bank + 1) * BANK_TILES)
+            nc.sync.dma_start(
+                out=a_raw[:].rearrange("p (t k) -> p t k", t=A_TILES)[:, tiles, :],
+                in_=anchor.rearrange("(t p) k -> p t k", p=P)[:, tiles, :],
+            )
         p_raw = keep.tile([P, (N_P // P) * D], BF16)
         load_cols = ROW_TILES * D
         pos_loads = pos.rearrange("(c p r) k -> c p (r k)", p=P, r=ROW_TILES)
@@ -54,9 +57,12 @@ def tile_crossgenderinfonceloss_pa_t_kernel(tc, anchor, pos, out):
 
         identity = keep.tile([P, P], F32)
         make_identity(nc, identity[:])
-        ones = keep.tile([P, 1], F32)
-        nc.vector.memset(ones[:], 1.0)
-        nc.scalar.activation(out=ones[:], in_=ones[:], func=ACT.Ln)
+        mask = keep.tile([P, P], F32)
+        nc.gpsimd.memset(mask[:], 0.0)
+        nc.gpsimd.affine_select(
+            out=mask[:], in_=mask[:], pattern=[[-1, P]], compare_op=ALU.not_equal,
+            fill=MASKED, base=0, channel_multiplier=1,
+        )
         result = keep.tile([P, P], F32)
         nc.vector.memset(result[:], 0.0)
 
@@ -93,10 +99,9 @@ def tile_crossgenderinfonceloss_pa_t_kernel(tc, anchor, pos, out):
         def quantise(codes, scales, grouped):
             nc.vector.quantize_mx(out=codes.bitcast(FP8X4), scales=scales, in_=grouped[:])
 
-        def score(t, moving_codes, moving_scales):
-            acc = psum_scores.tile([P, BLOCK], F32, name="acc")
+        def score(t, scores, moving_codes, moving_scales):
             nc.tensor.matmul_mx(
-                out=acc[:],
+                out=scores,
                 lhsT=a_codes[:, t * P : (t + 1) * P].bitcast(FP8X4),
                 lhsT_scale=a_scales[:, t * P : (t + 1) * P],
                 rhs=moving_codes.bitcast(FP8X4),
@@ -104,25 +109,54 @@ def tile_crossgenderinfonceloss_pa_t_kernel(tc, anchor, pos, out):
                 start=True,
                 stop=True,
             )
-            return acc
 
-        def find_largest(s, t, x):
-            nc.vector.tensor_reduce(out=largest[:, s, t : t + 1], in_=x[:], axis=AXIS.X, op=ALU.max)
+        def new_scores():
+            return psum_scores.tile([P, BLOCK], F32, name="scores")
 
-        def scale_largest(s, first, count):
-            tiles = slice(first, first + count)
+        def find_largest(s, tiles, x):
+            nc.vector.tensor_reduce(out=largest[:, s, tiles], in_=x, axis=AXIS.X, op=ALU.max)
+
+        def scale_largest(s, tiles):
             nc.gpsimd.tensor_scalar(
                 out=lowest[:, tiles, s], in0=largest[:, s, tiles],
                 scalar1=-1.0 / TEMPERATURE, scalar2=0.0, op0=ALU.mult, op1=ALU.add,
             )
 
         def exponential(s, t, x):
-            weights = stage.tile([P, BLOCK], F32, name="weights")
+            terms = stage.tile([P, BLOCK], F32, name="terms")
             nc.scalar.activation(
-                out=weights[:], in_=x[:], func=ACT.Exp,
+                out=terms[:, 0 : x.shape[1]], in_=x, func=ACT.Exp,
                 bias=lowest[:, t, s : s + 1], scale=1.0 / TEMPERATURE,
                 accum_out=sums[:, t, s : s + 1],
             )
+
+        ALL, POSITIVES = 0, 1
+        LAST = N_STATS - 1
+        both = [P, A_TILES, 2, N_STATS]
+        low = keep.tile([P, A_TILES, 2], F32)
+        shift = keep.tile([P, A_TILES], F32)
+        weight = keep.tile(both, F32)
+        earlier = keep.tile([P, A_TILES, 2], F32)
+        weighted = keep.tile([P, A_TILES, 2, LAST], F32)
+        lse = keep.tile([P, A_TILES, 2], F32)
+
+        def weigh():
+            nc.vector.tensor_reduce(out=low[:, :, ALL], in_=lowest[:], axis=AXIS.X, op=ALU.min)
+            nc.vector.tensor_reduce(
+                out=low[:, :, POSITIVES], in_=lowest[:, :, FIRST_BLOCK:N_STATS], axis=AXIS.X, op=ALU.min
+            )
+            nc.vector.tensor_tensor(
+                out=weight[:], in0=low[:].unsqueeze(3).to_broadcast(both),
+                in1=lowest[:].unsqueeze(2).to_broadcast(both), op=ALU.subtract,
+            )
+            nc.vector.memset(weight[:, :, POSITIVES, 0:FIRST_BLOCK], MASKED)
+            nc.scalar.activation(out=weight[:], in_=weight[:], func=ACT.Exp)
+            nc.vector.tensor_sub(out=shift[:], in0=low[:, :, ALL], in1=low[:, :, POSITIVES])
+            nc.vector.tensor_mul(
+                out=weighted[:], in0=weight[:, :, :, 0:LAST],
+                in1=sums[:, :, 0:LAST].unsqueeze(2).to_broadcast([P, A_TILES, 2, LAST]),
+            )
+            nc.vector.tensor_reduce(out=earlier[:], in_=weighted[:], axis=AXIS.X, op=ALU.add)
 
         def block_words(b):
             return p_raw_words[:, b * ROW_TILES : (b + 1) * ROW_TILES, :]
@@ -131,73 +165,79 @@ def tile_crossgenderinfonceloss_pa_t_kernel(tc, anchor, pos, out):
             cols = slice(b * BLOCK, (b + 1) * BLOCK)
             quantise(p_codes[:, cols], p_scales[:, cols], grouped)
 
+        def score_block(b):
+            cols = slice(b * BLOCK, (b + 1) * BLOCK)
+            accs = []
+            for t in range(A_TILES):
+                acc = new_scores()
+                score(t, acc[:], p_codes[:, cols], p_scales[:, cols])
+                accs.append(acc)
+            return accs
+
+        def score_anchors():
+            accs = []
+            for t in range(A_TILES):
+                acc = new_scores()
+                for place in range(A_TILES):
+                    other = (t + place) % A_TILES
+                    cols = slice(other * P, (other + 1) * P)
+                    score(t, acc[:, place * P : (place + 1) * P], a_codes[:, cols], a_scales[:, cols])
+                accs.append(acc)
+            return accs
+
         a_banks = transposes(a_raw_words)
         a_grouped = new_grouped()
         empty_bank(nc.scalar.copy, a_grouped, a_banks, 0)
         empty_bank(nc.vector.tensor_copy, a_grouped, a_banks, 1)
-        banks = transposes(block_words(0))
-        grouped = {0: new_grouped()}
-        empty_bank(nc.scalar.copy, grouped[0], banks, 0)
         quantise(a_codes[:], a_scales[:], a_grouped)
-        empty_bank(nc.vector.tensor_copy, grouped[0], banks, 1)
-        quantise_block(0, grouped[0])
+        grouped = {}
+        for b in range(AHEAD - 1):
+            banks = transposes(block_words(b))
+            grouped[b] = new_grouped()
+            empty_bank(nc.scalar.copy, grouped[b], banks, 0)
+            if b == 0:
+                empty_bank(nc.scalar.copy, grouped[b], banks, 1)
+                quantise_block(b, grouped[b])
+            else:
+                empty_bank(nc.vector.tensor_copy, grouped[b], banks, 1)
 
-        negatives = []
+        own = keep.tile([P, A_TILES, P], F32)
+        for i in range(N_BLOCKS + 1):
+            b = max(i - 1, 0)
+            accs = score_anchors() if i == 1 else score_block(b)
+            ahead = i + AHEAD - 1
+            if ahead < N_BLOCKS:
+                banks = transposes(block_words(ahead))
+                grouped[ahead] = new_grouped()
+            for t in range(A_TILES):
+                tile_t = slice(t, t + 1)
+                if i == 1:
+                    find_largest(OTHER_TILES, tile_t, accs[t][:, P:BLOCK])
+                    nc.vector.tensor_add(out=own[:, t, :], in0=accs[t][:, 0:P], in1=mask[:])
+                    scale_largest(OTHER_TILES, tile_t)
+                    exponential(OTHER_TILES, t, accs[t][:, P:BLOCK])
+                else:
+                    find_largest(FIRST_BLOCK + b, tile_t, accs[t][:])
+                    scale_largest(FIRST_BLOCK + b, tile_t)
+                    if i == N_BLOCKS and t == A_TILES - 1:
+                        weigh()
+                    exponential(FIRST_BLOCK + b, t, accs[t][:])
+                if t % 2 == 1 and ahead < N_BLOCKS:
+                    on_vector = t == 3 and i % 3 != 2
+                    empty_bank(nc.vector.tensor_copy if on_vector else nc.scalar.copy, grouped[ahead], banks, t // 2)
+            if i == 1:
+                find_largest(OWN_TILE, slice(0, A_TILES), own[:])
+                scale_largest(OWN_TILE, slice(0, A_TILES))
+                for t in range(A_TILES):
+                    exponential(OWN_TILE, t, own[:, t, :])
+            if ahead - 1 < N_BLOCKS:
+                quantise_block(ahead - 1, grouped[ahead - 1])
+
         for t in range(A_TILES):
-            acc = score(t, a_codes[:], a_scales[:])
-            x = stage.tile([P, N_A], F32, name="x%d" % t, bufs=1)
-            nc.scalar.copy(out=x[:], in_=acc[:])
-            own = x[:, t * P : (t + 1) * P]
-            nc.gpsimd.affine_select(
-                out=own, in_=own, pattern=[[-1, P]], compare_op=ALU.not_equal,
-                fill=MASKED, base=0, channel_multiplier=1,
+            nc.vector.scalar_tensor_tensor(
+                out=lse[:, t, :], in0=weight[:, t, :, LAST], scalar=sums[:, t, LAST : LAST + 1],
+                in1=earlier[:, t, :], op0=ALU.mult, op1=ALU.add,
             )
-            negatives.append(x)
-        banks = transposes(block_words(1))
-        grouped[1] = new_grouped()
-        empty_bank(nc.scalar.copy, grouped[1], banks, 0)
-        empty_bank(nc.vector.tensor_copy, grouped[1], banks, 1)
-        for t in range(A_TILES):
-            find_largest(NEGATIVES, t, negatives[t])
-        scale_largest(NEGATIVES, 0, A_TILES)
-        for t in range(A_TILES):
-            exponential(NEGATIVES, t, negatives[t])
-
-        for b in range(N_BLOCKS):
-            cols = slice(b * BLOCK, (b + 1) * BLOCK)
-            accs = [score(t, p_codes[:, cols], p_scales[:, cols]) for t in range(A_TILES)]
-            if b + 2 < N_BLOCKS:
-                banks = transposes(block_words(b + 2))
-                grouped[b + 2] = new_grouped()
-            for pair in range(2):
-                for t in (2 * pair, 2 * pair + 1):
-                    find_largest(b, t, accs[t])
-                scale_largest(b, 2 * pair, 2)
-                if pair == 0 and b + 1 < N_BLOCKS:
-                    quantise_block(b + 1, grouped[b + 1])
-                for t in (2 * pair, 2 * pair + 1):
-                    exponential(b, t, accs[t])
-                if b + 2 < N_BLOCKS:
-                    on_vector = pair == 1 and b % 2 == 1
-                    empty_bank(nc.vector.tensor_copy if on_vector else nc.scalar.copy, grouped[b + 2], banks, pair)
-
-        ALL, POSITIVES = 0, 1
-        low = keep.tile([P, A_TILES, 2], F32)
-        nc.vector.tensor_reduce(out=low[:, :, ALL], in_=lowest[:], axis=AXIS.X, op=ALU.min)
-        nc.vector.tensor_reduce(out=low[:, :, POSITIVES], in_=lowest[:, :, 0:N_BLOCKS], axis=AXIS.X, op=ALU.min)
-        both = [P, A_TILES, 2, N_STATS]
-        weight = keep.tile(both, F32)
-        nc.vector.tensor_tensor(
-            out=weight[:], in0=low[:].unsqueeze(3).to_broadcast(both),
-            in1=lowest[:].unsqueeze(2).to_broadcast(both), op=ALU.subtract,
-        )
-        nc.vector.memset(weight[:, :, POSITIVES, NEGATIVES], MASKED)
-        shift = keep.tile([P, A_TILES], F32)
-        nc.vector.tensor_sub(out=shift[:], in0=low[:, :, ALL], in1=low[:, :, POSITIVES])
-        nc.scalar.activation(out=weight[:], in_=weight[:], func=ACT.Exp)
-        nc.vector.tensor_mul(out=weight[:], in0=weight[:], in1=sums[:].unsqueeze(2).to_broadcast(both))
-        lse = keep.tile([P, A_TILES, 2], F32)
-        nc.vector.tensor_reduce(out=lse[:], in_=weight[:], axis=AXIS.X, op=ALU.add)
         nc.scalar.activation(out=lse[:], in_=lse[:], func=ACT.Ln)
         nc.vector.tensor_sub(out=lse[:, :, POSITIVES], in0=lse[:, :, POSITIVES], in1=lse[:, :, ALL])
         nc.vector.tensor_add(out=result[:, 0:A_TILES], in0=lse[:, :, POSITIVES], in1=shift[:])

@@ -26,7 +26,6 @@ ROW_TILES = BLOCK // P
 OTHER_TILES, OWN_TILE, FIRST_BLOCK = 0, 1, 2
 N_STATS = FIRST_BLOCK + N_BLOCKS
 BANK_TILES = 2
-AHEAD = 3
 BANKS = ROW_TILES // BANK_TILES
 MASKED = -1.0e36
 
@@ -51,7 +50,13 @@ def tile_crossgenderinfonceloss_pa_t_kernel(tc, anchor, pos, out):
         load_cols = ROW_TILES * D
         pos_loads = pos.rearrange("(c p r) k -> c p (r k)", p=P, r=ROW_TILES)
         for c in range(N_BLOCKS):
-            nc.sync.dma_start(out=p_raw[:, c * load_cols : (c + 1) * load_cols], in_=pos_loads[c])
+            pieces = BANKS if c == 0 else 1
+            piece_cols = load_cols // pieces
+            for i in range(pieces):
+                piece = slice(i * piece_cols, (i + 1) * piece_cols)
+                nc.sync.dma_start(
+                    out=p_raw[:, c * load_cols : (c + 1) * load_cols][:, piece], in_=pos_loads[c][:, piece]
+                )
         a_raw_words = a_raw[:].bitcast(F32).rearrange("p (r w) -> p r w", w=WORDS)
         p_raw_words = p_raw[:].bitcast(F32).rearrange("p (r w) -> p r w", w=WORDS)
 
@@ -134,11 +139,13 @@ def tile_crossgenderinfonceloss_pa_t_kernel(tc, anchor, pos, out):
         LAST = N_STATS - 1
         both = [P, A_TILES, 2, N_STATS]
         low = keep.tile([P, A_TILES, 2], F32)
-        shift = keep.tile([P, A_TILES], F32)
+        shift = keep.tile([P, P], F32)
+        nc.vector.memset(shift[:], 0.0)
+        shift_rows = keep.tile([P, P], F32)
         weight = keep.tile(both, F32)
         earlier = keep.tile([P, A_TILES, 2], F32)
         weighted = keep.tile([P, A_TILES, 2, LAST], F32)
-        lse = keep.tile([P, A_TILES, 2], F32)
+        total = keep.tile([P, A_TILES, 2], F32)
 
         def weigh():
             nc.vector.tensor_reduce(out=low[:, :, ALL], in_=lowest[:], axis=AXIS.X, op=ALU.min)
@@ -151,7 +158,10 @@ def tile_crossgenderinfonceloss_pa_t_kernel(tc, anchor, pos, out):
             )
             nc.vector.memset(weight[:, :, POSITIVES, 0:FIRST_BLOCK], MASKED)
             nc.scalar.activation(out=weight[:], in_=weight[:], func=ACT.Exp)
-            nc.vector.tensor_sub(out=shift[:], in0=low[:, :, ALL], in1=low[:, :, POSITIVES])
+            nc.vector.tensor_sub(out=shift[:, 0:A_TILES], in0=low[:, :, ALL], in1=low[:, :, POSITIVES])
+            flipped = psum_words.tile([P, 2, BANK_TILES * P], F32, name="flipped")
+            nc.tensor.transpose(flipped[:, 0, 0:P], shift[:], identity[:])
+            nc.vector.tensor_copy(out=shift_rows[:], in_=flipped[:, 0, 0:P])
             nc.vector.tensor_mul(
                 out=weighted[:], in0=weight[:, :, :, 0:LAST],
                 in1=sums[:, :, 0:LAST].unsqueeze(2).to_broadcast([P, A_TILES, 2, LAST]),
@@ -174,9 +184,9 @@ def tile_crossgenderinfonceloss_pa_t_kernel(tc, anchor, pos, out):
                 accs.append(acc)
             return accs
 
-        def score_anchors():
+        def score_anchors(tiles):
             accs = []
-            for t in range(A_TILES):
+            for t in tiles:
                 acc = new_scores()
                 for place in range(A_TILES):
                     other = (t + place) % A_TILES
@@ -191,41 +201,41 @@ def tile_crossgenderinfonceloss_pa_t_kernel(tc, anchor, pos, out):
         empty_bank(nc.vector.tensor_copy, a_grouped, a_banks, 1)
         quantise(a_codes[:], a_scales[:], a_grouped)
         grouped = {}
-        for b in range(AHEAD - 1):
-            banks = transposes(block_words(b))
-            grouped[b] = new_grouped()
-            empty_bank(nc.scalar.copy, grouped[b], banks, 0)
-            if b == 0:
-                empty_bank(nc.scalar.copy, grouped[b], banks, 1)
-                quantise_block(b, grouped[b])
-            else:
-                empty_bank(nc.vector.tensor_copy, grouped[b], banks, 1)
+        grouped[0] = new_grouped()
+        grouped[1] = new_grouped()
+        banks = transposes(block_words(0))
+        for bank in range(BANKS):
+            empty_bank(nc.scalar.copy, grouped[0], banks, bank)
+        quantise_block(0, grouped[0])
+        anchor_accs = score_anchors(range(0, 2))
+        banks = transposes(block_words(1))
+        for bank in range(BANKS):
+            empty_bank(nc.scalar.copy, grouped[1], banks, bank)
+        anchor_accs += score_anchors(range(2, A_TILES))
 
         own = keep.tile([P, A_TILES, P], F32)
         for i in range(N_BLOCKS + 1):
-            b = max(i - 1, 0)
-            accs = score_anchors() if i == 1 else score_block(b)
-            ahead = i + AHEAD - 1
+            accs = anchor_accs if i == 0 else score_block(i - 1)
+            s = FIRST_BLOCK + i - 1
+            ahead = i + 2
             if ahead < N_BLOCKS:
                 banks = transposes(block_words(ahead))
                 grouped[ahead] = new_grouped()
             for t in range(A_TILES):
                 tile_t = slice(t, t + 1)
-                if i == 1:
+                if i == 0:
                     find_largest(OTHER_TILES, tile_t, accs[t][:, P:BLOCK])
                     nc.vector.tensor_add(out=own[:, t, :], in0=accs[t][:, 0:P], in1=mask[:])
                     scale_largest(OTHER_TILES, tile_t)
                     exponential(OTHER_TILES, t, accs[t][:, P:BLOCK])
                 else:
-                    find_largest(FIRST_BLOCK + b, tile_t, accs[t][:])
-                    scale_largest(FIRST_BLOCK + b, tile_t)
-                    if i == N_BLOCKS and t == A_TILES - 1:
-                        weigh()
-                    exponential(FIRST_BLOCK + b, t, accs[t][:])
+                    find_largest(s, tile_t, accs[t][:])
+                    scale_largest(s, tile_t)
+                    exponential(s, t, accs[t][:])
                 if t % 2 == 1 and ahead < N_BLOCKS:
-                    on_vector = t == 3 and i % 3 != 2
+                    on_vector = t == 3 and i % 2 == 1
                     empty_bank(nc.vector.tensor_copy if on_vector else nc.scalar.copy, grouped[ahead], banks, t // 2)
-            if i == 1:
+            if i == 0:
                 find_largest(OWN_TILE, slice(0, A_TILES), own[:])
                 scale_largest(OWN_TILE, slice(0, A_TILES))
                 for t in range(A_TILES):
@@ -233,17 +243,19 @@ def tile_crossgenderinfonceloss_pa_t_kernel(tc, anchor, pos, out):
             if ahead - 1 < N_BLOCKS:
                 quantise_block(ahead - 1, grouped[ahead - 1])
 
+        weigh()
         for t in range(A_TILES):
             nc.vector.scalar_tensor_tensor(
-                out=lse[:, t, :], in0=weight[:, t, :, LAST], scalar=sums[:, t, LAST : LAST + 1],
+                out=total[:, t, :], in0=weight[:, t, :, LAST], scalar=sums[:, t, LAST : LAST + 1],
                 in1=earlier[:, t, :], op0=ALU.mult, op1=ALU.add,
             )
-        nc.scalar.activation(out=lse[:], in_=lse[:], func=ACT.Ln)
-        nc.vector.tensor_sub(out=lse[:, :, POSITIVES], in0=lse[:, :, POSITIVES], in1=lse[:, :, ALL])
-        nc.vector.tensor_add(out=result[:, 0:A_TILES], in0=lse[:, :, POSITIVES], in1=shift[:])
+        ratio = keep.tile([P, A_TILES], F32)
+        nc.vector.reciprocal(out=ratio[:], in_=total[:, :, ALL])
+        nc.vector.tensor_mul(out=ratio[:], in0=ratio[:], in1=total[:, :, POSITIVES])
+        nc.scalar.activation(out=result[:, 0:A_TILES], in_=ratio[:], func=ACT.Ln)
 
-        result_rows_psum = psum_words.tile([P, P], F32, name="flipped")
-        nc.tensor.transpose(result_rows_psum[:], result[:], identity[:])
+        flipped = psum_words.tile([P, 2, BANK_TILES * P], F32, name="flipped")
+        nc.tensor.transpose(flipped[:, 0, 0:P], result[:], identity[:])
         result_rows = keep.tile([P, P], F32)
-        nc.vector.tensor_copy(out=result_rows[:], in_=result_rows_psum[:])
+        nc.vector.tensor_add(out=result_rows[:], in0=flipped[:, 0, 0:P], in1=shift_rows[:])
         nc.sync.dma_start(out=out.rearrange("(t p) -> t p", p=P), in_=result_rows[0:A_TILES, :])

@@ -35,8 +35,7 @@ def tile_crossgenderinfonceloss_pa_t_kernel(tc, anchor, pos, out):
     with ExitStack() as ctx:
         keep = ctx.enter_context(tc.tile_pool(name="keep", bufs=1))
         stage = ctx.enter_context(tc.tile_pool(name="stage", bufs=3))
-        psum_words = ctx.enter_context(tc.psum_pool(name="psum_words", bufs=3))
-        psum_scores = ctx.enter_context(tc.psum_pool(name="psum_scores", bufs=5))
+        psum = ctx.enter_context(tc.psum_pool(name="psum", bufs=8))
         ctx.enter_context(tc.manual_schedule())
 
         a_raw = keep.tile([P, A_TILES * D], BF16)
@@ -68,8 +67,8 @@ def tile_crossgenderinfonceloss_pa_t_kernel(tc, anchor, pos, out):
             out=mask[:], in_=mask[:], pattern=[[-1, P]], compare_op=ALU.not_equal,
             fill=MASKED, base=0, channel_multiplier=1,
         )
-        result = keep.tile([P, P], F32)
-        nc.vector.memset(result[:], 0.0)
+        ratio = keep.tile([P, P], F32)
+        nc.vector.memset(ratio[:], 1.0)
 
         a_codes = keep.tile([P, N_A], U32, align_bytes=64)
         a_scales = keep.tile([P, N_A], U8, align_bytes=64)
@@ -79,10 +78,13 @@ def tile_crossgenderinfonceloss_pa_t_kernel(tc, anchor, pos, out):
         lowest = keep.tile([P, A_TILES, N_STATS], F32)
         sums = keep.tile([P, A_TILES, N_STATS], F32)
 
+        def new_words():
+            return psum.tile([P, 2, BANK_TILES * P], F32, name="bank")
+
         def transposes(raw_words):
             banks = []
             for bank in range(BANKS):
-                flipped = psum_words.tile([P, 2, BANK_TILES * P], F32, name="flipped")
+                flipped = new_words()
                 for u in range(2):
                     for i in range(BANK_TILES):
                         nc.tensor.transpose(
@@ -102,7 +104,7 @@ def tile_crossgenderinfonceloss_pa_t_kernel(tc, anchor, pos, out):
             copy(out=words[:, rows, :], in_=banks[bank][:].rearrange("p u c -> p c u"))
 
         def quantise(codes, scales, grouped):
-            nc.vector.quantize_mx(out=codes.bitcast(FP8X4), scales=scales, in_=grouped[:])
+            nc.vector.quantize_mx(out=codes.bitcast(FP8X4), scales=scales, in_=grouped)
 
         def score(t, scores, moving_codes, moving_scales):
             nc.tensor.matmul_mx(
@@ -116,7 +118,7 @@ def tile_crossgenderinfonceloss_pa_t_kernel(tc, anchor, pos, out):
             )
 
         def new_scores():
-            return psum_scores.tile([P, BLOCK], F32, name="scores")
+            return psum.tile([P, BLOCK], F32, name="bank")
 
         def find_largest(s, tiles, x):
             nc.vector.tensor_reduce(out=largest[:, s, tiles], in_=x, axis=AXIS.X, op=ALU.max)
@@ -136,15 +138,11 @@ def tile_crossgenderinfonceloss_pa_t_kernel(tc, anchor, pos, out):
             )
 
         ALL, POSITIVES = 0, 1
-        LAST = N_STATS - 1
         both = [P, A_TILES, 2, N_STATS]
         low = keep.tile([P, A_TILES, 2], F32)
         shift = keep.tile([P, P], F32)
         nc.vector.memset(shift[:], 0.0)
-        shift_rows = keep.tile([P, P], F32)
         weight = keep.tile(both, F32)
-        earlier = keep.tile([P, A_TILES, 2], F32)
-        weighted = keep.tile([P, A_TILES, 2, LAST], F32)
         total = keep.tile([P, A_TILES, 2], F32)
 
         def weigh():
@@ -159,21 +157,15 @@ def tile_crossgenderinfonceloss_pa_t_kernel(tc, anchor, pos, out):
             nc.vector.memset(weight[:, :, POSITIVES, 0:FIRST_BLOCK], MASKED)
             nc.scalar.activation(out=weight[:], in_=weight[:], func=ACT.Exp)
             nc.vector.tensor_sub(out=shift[:, 0:A_TILES], in0=low[:, :, ALL], in1=low[:, :, POSITIVES])
-            flipped = psum_words.tile([P, 2, BANK_TILES * P], F32, name="flipped")
-            nc.tensor.transpose(flipped[:, 0, 0:P], shift[:], identity[:])
-            nc.vector.tensor_copy(out=shift_rows[:], in_=flipped[:, 0, 0:P])
-            nc.vector.tensor_mul(
-                out=weighted[:], in0=weight[:, :, :, 0:LAST],
-                in1=sums[:, :, 0:LAST].unsqueeze(2).to_broadcast([P, A_TILES, 2, LAST]),
-            )
-            nc.vector.tensor_reduce(out=earlier[:], in_=weighted[:], axis=AXIS.X, op=ALU.add)
+            nc.vector.tensor_mul(out=weight[:], in0=weight[:], in1=sums[:].unsqueeze(2).to_broadcast(both))
+            nc.vector.tensor_reduce(out=total[:], in_=weight[:], axis=AXIS.X, op=ALU.add)
 
         def block_words(b):
             return p_raw_words[:, b * ROW_TILES : (b + 1) * ROW_TILES, :]
 
         def quantise_block(b, grouped):
             cols = slice(b * BLOCK, (b + 1) * BLOCK)
-            quantise(p_codes[:, cols], p_scales[:, cols], grouped)
+            quantise(p_codes[:, cols], p_scales[:, cols], grouped[:])
 
         def score_block(b):
             cols = slice(b * BLOCK, (b + 1) * BLOCK)
@@ -195,25 +187,35 @@ def tile_crossgenderinfonceloss_pa_t_kernel(tc, anchor, pos, out):
                 accs.append(acc)
             return accs
 
+        own = keep.tile([P, A_TILES, P], F32)
+
+        def reduce_anchors(t, acc):
+            find_largest(OTHER_TILES, slice(t, t + 1), acc[:, P:BLOCK])
+            nc.vector.tensor_add(out=own[:, t, :], in0=acc[:, 0:P], in1=mask[:])
+            scale_largest(OTHER_TILES, slice(t, t + 1))
+
         a_banks = transposes(a_raw_words)
         a_grouped = new_grouped()
-        empty_bank(nc.scalar.copy, a_grouped, a_banks, 0)
-        empty_bank(nc.vector.tensor_copy, a_grouped, a_banks, 1)
-        quantise(a_codes[:], a_scales[:], a_grouped)
+        half = N_A // BANKS
+        for bank in range(BANKS):
+            empty_bank(nc.scalar.copy, a_grouped, a_banks, bank)
+            cols = slice(bank * half, (bank + 1) * half)
+            quantise(a_codes[:, cols], a_scales[:, cols], a_grouped[:, cols.start * PACK : cols.stop * PACK])
         grouped = {}
         grouped[0] = new_grouped()
         grouped[1] = new_grouped()
         banks = transposes(block_words(0))
         for bank in range(BANKS):
             empty_bank(nc.scalar.copy, grouped[0], banks, bank)
-        quantise_block(0, grouped[0])
         anchor_accs = score_anchors(range(0, 2))
+        reduce_anchors(0, anchor_accs[0])
+        quantise_block(0, grouped[0])
         banks = transposes(block_words(1))
+        exponential(OTHER_TILES, 0, anchor_accs[0][:, P:BLOCK])
         for bank in range(BANKS):
             empty_bank(nc.scalar.copy, grouped[1], banks, bank)
         anchor_accs += score_anchors(range(2, A_TILES))
 
-        own = keep.tile([P, A_TILES, P], F32)
         for i in range(N_BLOCKS + 1):
             accs = anchor_accs if i == 0 else score_block(i - 1)
             s = FIRST_BLOCK + i - 1
@@ -224,10 +226,9 @@ def tile_crossgenderinfonceloss_pa_t_kernel(tc, anchor, pos, out):
             for t in range(A_TILES):
                 tile_t = slice(t, t + 1)
                 if i == 0:
-                    find_largest(OTHER_TILES, tile_t, accs[t][:, P:BLOCK])
-                    nc.vector.tensor_add(out=own[:, t, :], in0=accs[t][:, 0:P], in1=mask[:])
-                    scale_largest(OTHER_TILES, tile_t)
-                    exponential(OTHER_TILES, t, accs[t][:, P:BLOCK])
+                    if t > 0:
+                        reduce_anchors(t, accs[t])
+                        exponential(OTHER_TILES, t, accs[t][:, P:BLOCK])
                 else:
                     find_largest(s, tile_t, accs[t][:])
                     scale_largest(s, tile_t)
@@ -244,18 +245,15 @@ def tile_crossgenderinfonceloss_pa_t_kernel(tc, anchor, pos, out):
                 quantise_block(ahead - 1, grouped[ahead - 1])
 
         weigh()
-        for t in range(A_TILES):
-            nc.vector.scalar_tensor_tensor(
-                out=total[:, t, :], in0=weight[:, t, :, LAST], scalar=sums[:, t, LAST : LAST + 1],
-                in1=earlier[:, t, :], op0=ALU.mult, op1=ALU.add,
-            )
-        ratio = keep.tile([P, A_TILES], F32)
-        nc.vector.reciprocal(out=ratio[:], in_=total[:, :, ALL])
-        nc.vector.tensor_mul(out=ratio[:], in0=ratio[:], in1=total[:, :, POSITIVES])
-        nc.scalar.activation(out=result[:, 0:A_TILES], in_=ratio[:], func=ACT.Ln)
+        inverse = keep.tile([P, A_TILES], F32)
+        nc.vector.reciprocal(out=inverse[:], in_=total[:, :, ALL])
+        nc.vector.tensor_mul(out=ratio[:, 0:A_TILES], in0=inverse[:], in1=total[:, :, POSITIVES])
 
-        flipped = psum_words.tile([P, 2, BANK_TILES * P], F32, name="flipped")
-        nc.tensor.transpose(flipped[:, 0, 0:P], result[:], identity[:])
+        shift_rows = new_words()
+        nc.tensor.transpose(shift_rows[:, 0, 0:P], shift[:], identity[:])
+        ratio_rows = new_words()
+        nc.tensor.transpose(ratio_rows[:, 0, 0:P], ratio[:], identity[:])
         result_rows = keep.tile([P, P], F32)
-        nc.vector.tensor_add(out=result_rows[:], in0=flipped[:, 0, 0:P], in1=shift_rows[:])
+        nc.scalar.activation(out=result_rows[:], in_=ratio_rows[:, 0, 0:P], func=ACT.Ln)
+        nc.vector.tensor_add(out=result_rows[:], in0=result_rows[:], in1=shift_rows[:, 0, 0:P])
         nc.sync.dma_start(out=out.rearrange("(t p) -> t p", p=P), in_=result_rows[0:A_TILES, :])

@@ -27,6 +27,7 @@ OTHER_TILES, OWN_TILE, FIRST_BLOCK = 0, 1, 2
 N_STATS = FIRST_BLOCK + N_BLOCKS
 BANK_TILES = 2
 BANKS = ROW_TILES // BANK_TILES
+WARM_UP = 12
 MASKED = -1.0e36
 
 
@@ -39,12 +40,8 @@ def tile_crossgenderinfonceloss_pa_t_kernel(tc, anchor, pos, out):
         ctx.enter_context(tc.manual_schedule())
 
         a_raw = keep.tile([P, A_TILES * D], BF16)
-        for bank in range(BANKS):
-            tiles = slice(bank * BANK_TILES, (bank + 1) * BANK_TILES)
-            nc.sync.dma_start(
-                out=a_raw[:].rearrange("p (t k) -> p t k", t=A_TILES)[:, tiles, :],
-                in_=anchor.rearrange("(t p) k -> p t k", p=P)[:, tiles, :],
-            )
+        for t in range(A_TILES):
+            nc.sync.dma_start(out=a_raw[:, t * D : (t + 1) * D], in_=anchor[t * P : (t + 1) * P, :])
         p_raw = keep.tile([P, (N_P // P) * D], BF16)
         load_cols = ROW_TILES * D
         pos_loads = pos.rearrange("(c p r) k -> c p (r k)", p=P, r=ROW_TILES)
@@ -59,6 +56,8 @@ def tile_crossgenderinfonceloss_pa_t_kernel(tc, anchor, pos, out):
         a_raw_words = a_raw[:].bitcast(F32).rearrange("p (r w) -> p r w", w=WORDS)
         p_raw_words = p_raw[:].bitcast(F32).rearrange("p (r w) -> p r w", w=WORDS)
 
+        zeros = keep.tile([P, P], BF16)
+        nc.vector.memset(zeros[:], 0.0)
         identity = keep.tile([P, P], F32)
         make_identity(nc, identity[:])
         mask = keep.tile([P, P], F32)
@@ -81,27 +80,24 @@ def tile_crossgenderinfonceloss_pa_t_kernel(tc, anchor, pos, out):
         def new_words():
             return psum.tile([P, 2, BANK_TILES * P], F32, name="bank")
 
-        def transposes(raw_words):
-            banks = []
-            for bank in range(BANKS):
-                flipped = new_words()
+        def transposes(raw_words, bank):
+            flipped = new_words()
+            for i in range(BANK_TILES):
                 for u in range(2):
-                    for i in range(BANK_TILES):
-                        nc.tensor.transpose(
-                            flipped[:, u, i * P : (i + 1) * P],
-                            raw_words[:, bank * BANK_TILES + i, u:WORDS:2],
-                            identity[:],
-                        )
-                banks.append(flipped)
-            return banks
+                    nc.tensor.transpose(
+                        flipped[:, u, i * P : (i + 1) * P],
+                        raw_words[:, bank * BANK_TILES + i, u:WORDS:2],
+                        identity[:],
+                    )
+            return flipped
 
         def new_grouped():
             return stage.tile([P, BLOCK * PACK], BF16, name="grouped", align_bytes=64)
 
-        def empty_bank(copy, grouped, banks, bank):
+        def empty_bank(copy, grouped, bank, flipped):
             words = grouped[:].bitcast(F32).rearrange("p (c u) -> p c u", u=2)
             rows = slice(bank * BANK_TILES * P, (bank + 1) * BANK_TILES * P)
-            copy(out=words[:, rows, :], in_=banks[bank][:].rearrange("p u c -> p c u"))
+            copy(out=words[:, rows, :], in_=flipped[:].rearrange("p u c -> p c u"))
 
         def quantise(codes, scales, grouped):
             nc.vector.quantize_mx(out=codes.bitcast(FP8X4), scales=scales, in_=grouped)
@@ -194,26 +190,29 @@ def tile_crossgenderinfonceloss_pa_t_kernel(tc, anchor, pos, out):
             nc.vector.tensor_add(out=own[:, t, :], in0=acc[:, 0:P], in1=mask[:])
             scale_largest(OTHER_TILES, slice(t, t + 1))
 
-        a_banks = transposes(a_raw_words)
+        idle = new_words()
+        for i in range(WARM_UP):
+            nc.tensor.matmul(idle[:, 0, 0:P], zeros[:], zeros[:], start=True, stop=True)
+
         a_grouped = new_grouped()
+        a_banks = [transposes(a_raw_words, bank) for bank in range(BANKS)]
         half = N_A // BANKS
         for bank in range(BANKS):
-            empty_bank(nc.scalar.copy, a_grouped, a_banks, bank)
+            empty_bank(nc.scalar.copy, a_grouped, bank, a_banks[bank])
             cols = slice(bank * half, (bank + 1) * half)
             quantise(a_codes[:, cols], a_scales[:, cols], a_grouped[:, cols.start * PACK : cols.stop * PACK])
         grouped = {}
         grouped[0] = new_grouped()
         grouped[1] = new_grouped()
-        banks = transposes(block_words(0))
         for bank in range(BANKS):
-            empty_bank(nc.scalar.copy, grouped[0], banks, bank)
-        anchor_accs = score_anchors(range(0, 2))
+            empty_bank(nc.scalar.copy, grouped[0], bank, transposes(block_words(0), bank))
+        anchor_accs = score_anchors(range(0, 1))
         reduce_anchors(0, anchor_accs[0])
         quantise_block(0, grouped[0])
-        banks = transposes(block_words(1))
+        empty_bank(nc.scalar.copy, grouped[1], 0, transposes(block_words(1), 0))
         exponential(OTHER_TILES, 0, anchor_accs[0][:, P:BLOCK])
-        for bank in range(BANKS):
-            empty_bank(nc.scalar.copy, grouped[1], banks, bank)
+        anchor_accs += score_anchors(range(1, 2))
+        empty_bank(nc.scalar.copy, grouped[1], 1, transposes(block_words(1), 1))
         anchor_accs += score_anchors(range(2, A_TILES))
 
         for i in range(N_BLOCKS + 1):
@@ -221,7 +220,7 @@ def tile_crossgenderinfonceloss_pa_t_kernel(tc, anchor, pos, out):
             s = FIRST_BLOCK + i - 1
             ahead = i + 2
             if ahead < N_BLOCKS:
-                banks = transposes(block_words(ahead))
+                banks = [transposes(block_words(ahead), bank) for bank in range(BANKS)]
                 grouped[ahead] = new_grouped()
             for t in range(A_TILES):
                 tile_t = slice(t, t + 1)
@@ -234,8 +233,11 @@ def tile_crossgenderinfonceloss_pa_t_kernel(tc, anchor, pos, out):
                     scale_largest(s, tile_t)
                     exponential(s, t, accs[t][:])
                 if t % 2 == 1 and ahead < N_BLOCKS:
-                    on_vector = t == 3 and i % 2 == 1
-                    empty_bank(nc.vector.tensor_copy if on_vector else nc.scalar.copy, grouped[ahead], banks, t // 2)
+                    bank = t // 2
+                    on_vector = bank == 1 and i % 2 == 1
+                    empty_bank(
+                        nc.vector.tensor_copy if on_vector else nc.scalar.copy, grouped[ahead], bank, banks[bank]
+                    )
             if i == 0:
                 find_largest(OWN_TILE, slice(0, A_TILES), own[:])
                 scale_largest(OWN_TILE, slice(0, A_TILES))

@@ -27,7 +27,6 @@ OTHER_TILES, OWN_TILE, FIRST_BLOCK = 0, 1, 2
 N_STATS = FIRST_BLOCK + N_BLOCKS
 BANK_TILES = 2
 BANKS = ROW_TILES // BANK_TILES
-WARM_UP = 12
 MASKED = -1.0e36
 
 
@@ -56,8 +55,6 @@ def tile_crossgenderinfonceloss_pa_t_kernel(tc, anchor, pos, out):
         a_raw_words = a_raw[:].bitcast(F32).rearrange("p (r w) -> p r w", w=WORDS)
         p_raw_words = p_raw[:].bitcast(F32).rearrange("p (r w) -> p r w", w=WORDS)
 
-        zeros = keep.tile([P, P], BF16)
-        nc.vector.memset(zeros[:], 0.0)
         identity = keep.tile([P, P], F32)
         make_identity(nc, identity[:])
         mask = keep.tile([P, P], F32)
@@ -172,9 +169,9 @@ def tile_crossgenderinfonceloss_pa_t_kernel(tc, anchor, pos, out):
                 accs.append(acc)
             return accs
 
-        def score_anchors(tiles):
+        def score_anchors():
             accs = []
-            for t in tiles:
+            for t in range(A_TILES):
                 acc = new_scores()
                 for place in range(A_TILES):
                     other = (t + place) % A_TILES
@@ -190,10 +187,6 @@ def tile_crossgenderinfonceloss_pa_t_kernel(tc, anchor, pos, out):
             nc.vector.tensor_add(out=own[:, t, :], in0=acc[:, 0:P], in1=mask[:])
             scale_largest(OTHER_TILES, slice(t, t + 1))
 
-        idle = new_words()
-        for i in range(WARM_UP):
-            nc.tensor.matmul(idle[:, 0, 0:P], zeros[:], zeros[:], start=True, stop=True)
-
         a_grouped = new_grouped()
         a_banks = [transposes(a_raw_words, bank) for bank in range(BANKS)]
         half = N_A // BANKS
@@ -206,14 +199,13 @@ def tile_crossgenderinfonceloss_pa_t_kernel(tc, anchor, pos, out):
         grouped[1] = new_grouped()
         for bank in range(BANKS):
             empty_bank(nc.scalar.copy, grouped[0], bank, transposes(block_words(0), bank))
-        anchor_accs = score_anchors(range(0, 1))
-        reduce_anchors(0, anchor_accs[0])
+        anchor_accs = score_anchors()
+        for t in range(2):
+            reduce_anchors(t, anchor_accs[t])
+            exponential(OTHER_TILES, t, anchor_accs[t][:, P:BLOCK])
         quantise_block(0, grouped[0])
-        empty_bank(nc.scalar.copy, grouped[1], 0, transposes(block_words(1), 0))
-        exponential(OTHER_TILES, 0, anchor_accs[0][:, P:BLOCK])
-        anchor_accs += score_anchors(range(1, 2))
-        empty_bank(nc.scalar.copy, grouped[1], 1, transposes(block_words(1), 1))
-        anchor_accs += score_anchors(range(2, A_TILES))
+        for bank in range(BANKS):
+            empty_bank(nc.scalar.copy, grouped[1], bank, transposes(block_words(1), bank))
 
         for i in range(N_BLOCKS + 1):
             accs = anchor_accs if i == 0 else score_block(i - 1)
@@ -225,7 +217,7 @@ def tile_crossgenderinfonceloss_pa_t_kernel(tc, anchor, pos, out):
             for t in range(A_TILES):
                 tile_t = slice(t, t + 1)
                 if i == 0:
-                    if t > 0:
+                    if t > 1:
                         reduce_anchors(t, accs[t])
                         exponential(OTHER_TILES, t, accs[t][:, P:BLOCK])
                 else:

from contextlib import ExitStack

import concourse.mybir as mybir
from concourse.masks import make_identity

F32 = mybir.dt.float32
BF16 = mybir.dt.bfloat16
U32 = mybir.dt.uint32
U8 = mybir.dt.uint8
FP8X4 = mybir.dt.float8_e4m3fn_x4
ALU = mybir.AluOpType
ACT = mybir.ActivationFunctionType
AXIS = mybir.AxisListType

P = 128
N_A, N_P, D = 512, 8192, 512
TEMPERATURE = 0.07
FLOPS = 2 * N_A * D * (N_P + N_A)

PACK = 4
WORDS = D // 2
A_TILES = N_A // P
BLOCK = 512
N_BLOCKS = N_P // BLOCK
ROW_TILES = BLOCK // P
OTHER_TILES, OWN_TILE, FIRST_BLOCK = 0, 1, 2
N_STATS = FIRST_BLOCK + N_BLOCKS
BANK_TILES = 2
BANKS = ROW_TILES // BANK_TILES
MASKED = -1.0e36


def tile_crossgenderinfonceloss_pa_t_kernel(tc, anchor, pos, out):
    nc = tc.nc
    with ExitStack() as ctx:
        keep = ctx.enter_context(tc.tile_pool(name="keep", bufs=1))
        stage = ctx.enter_context(tc.tile_pool(name="stage", bufs=3))
        psum = ctx.enter_context(tc.psum_pool(name="psum", bufs=8))
        ctx.enter_context(tc.manual_schedule())

        a_raw = keep.tile([P, A_TILES * D], BF16)
        for t in range(A_TILES):
            nc.sync.dma_start(out=a_raw[:, t * D : (t + 1) * D], in_=anchor[t * P : (t + 1) * P, :])
        p_raw = keep.tile([P, (N_P // P) * D], BF16)
        load_cols = ROW_TILES * D
        pos_loads = pos.rearrange("(c p r) k -> c p (r k)", p=P, r=ROW_TILES)
        for c in range(N_BLOCKS):
            pieces = BANKS if c == 0 else 1
            piece_cols = load_cols // pieces
            for i in range(pieces):
                piece = slice(i * piece_cols, (i + 1) * piece_cols)
                nc.sync.dma_start(
                    out=p_raw[:, c * load_cols : (c + 1) * load_cols][:, piece], in_=pos_loads[c][:, piece]
                )
        a_raw_words = a_raw[:].bitcast(F32).rearrange("p (r w) -> p r w", w=WORDS)
        p_raw_words = p_raw[:].bitcast(F32).rearrange("p (r w) -> p r w", w=WORDS)

        identity = keep.tile([P, P], F32)
        make_identity(nc, identity[:])
        mask = keep.tile([P, P], F32)
        nc.gpsimd.memset(mask[:], 0.0)
        nc.gpsimd.affine_select(
            out=mask[:], in_=mask[:], pattern=[[-1, P]], compare_op=ALU.not_equal,
            fill=MASKED, base=0, channel_multiplier=1,
        )
        ratio = keep.tile([P, P], F32)
        nc.vector.memset(ratio[:], 1.0)

        a_codes = keep.tile([P, N_A], U32, align_bytes=64)
        a_scales = keep.tile([P, N_A], U8, align_bytes=64)
        p_codes = keep.tile([P, N_P], U32, align_bytes=64)
        p_scales = keep.tile([P, N_P], U8, align_bytes=64)
        largest = keep.tile([P, N_STATS, A_TILES], F32)
        lowest = keep.tile([P, A_TILES, N_STATS], F32)
        sums = keep.tile([P, A_TILES, N_STATS], F32)

        def new_words():
            return psum.tile([P, 2, BANK_TILES * P], F32, name="bank")

        def transposes(raw_words, bank):
            flipped = new_words()
            for i in range(BANK_TILES):
                for u in range(2):
                    nc.tensor.transpose(
                        flipped[:, u, i * P : (i + 1) * P],
                        raw_words[:, bank * BANK_TILES + i, u:WORDS:2],
                        identity[:],
                    )
            return flipped

        def new_grouped():
            return stage.tile([P, BLOCK * PACK], BF16, name="grouped", align_bytes=64)

        def empty_bank(copy, grouped, bank, flipped):
            words = grouped[:].bitcast(F32).rearrange("p (c u) -> p c u", u=2)
            rows = slice(bank * BANK_TILES * P, (bank + 1) * BANK_TILES * P)
            copy(out=words[:, rows, :], in_=flipped[:].rearrange("p u c -> p c u"))

        def quantise(codes, scales, grouped):
            nc.vector.quantize_mx(out=codes.bitcast(FP8X4), scales=scales, in_=grouped)

        def score(t, scores, moving_codes, moving_scales):
            nc.tensor.matmul_mx(
                out=scores,
                lhsT=a_codes[:, t * P : (t + 1) * P].bitcast(FP8X4),
                lhsT_scale=a_scales[:, t * P : (t + 1) * P],
                rhs=moving_codes.bitcast(FP8X4),
                rhs_scale=moving_scales,
                start=True,
                stop=True,
            )

        def new_scores():
            return psum.tile([P, BLOCK], F32, name="bank")

        def find_largest(s, tiles, x):
            nc.vector.tensor_reduce(out=largest[:, s, tiles], in_=x, axis=AXIS.X, op=ALU.max)

        def scale_largest(s, tiles):
            nc.gpsimd.tensor_scalar(
                out=lowest[:, tiles, s], in0=largest[:, s, tiles],
                scalar1=-1.0 / TEMPERATURE, scalar2=0.0, op0=ALU.mult, op1=ALU.add,
            )

        def exponential(s, t, x):
            terms = stage.tile([P, BLOCK], F32, name="terms")
            nc.scalar.activation(
                out=terms[:, 0 : x.shape[1]], in_=x, func=ACT.Exp,
                bias=lowest[:, t, s : s + 1], scale=1.0 / TEMPERATURE,
                accum_out=sums[:, t, s : s + 1],
            )

        ALL, POSITIVES = 0, 1
        both = [P, A_TILES, 2, N_STATS]
        low = keep.tile([P, A_TILES, 2], F32)
        shift = keep.tile([P, P], F32)
        nc.vector.memset(shift[:], 0.0)
        weight = keep.tile(both, F32)
        total = keep.tile([P, A_TILES, 2], F32)

        def weigh():
            nc.vector.tensor_reduce(out=low[:, :, ALL], in_=lowest[:], axis=AXIS.X, op=ALU.min)
            nc.vector.tensor_reduce(
                out=low[:, :, POSITIVES], in_=lowest[:, :, FIRST_BLOCK:N_STATS], axis=AXIS.X, op=ALU.min
            )
            nc.vector.tensor_tensor(
                out=weight[:], in0=low[:].unsqueeze(3).to_broadcast(both),
                in1=lowest[:].unsqueeze(2).to_broadcast(both), op=ALU.subtract,
            )
            nc.vector.memset(weight[:, :, POSITIVES, 0:FIRST_BLOCK], MASKED)
            nc.scalar.activation(out=weight[:], in_=weight[:], func=ACT.Exp)
            nc.vector.tensor_sub(out=shift[:, 0:A_TILES], in0=low[:, :, ALL], in1=low[:, :, POSITIVES])
            nc.vector.tensor_mul(out=weight[:], in0=weight[:], in1=sums[:].unsqueeze(2).to_broadcast(both))
            nc.vector.tensor_reduce(out=total[:], in_=weight[:], axis=AXIS.X, op=ALU.add)

        def block_words(b):
            return p_raw_words[:, b * ROW_TILES : (b + 1) * ROW_TILES, :]

        def quantise_block(b, grouped):
            cols = slice(b * BLOCK, (b + 1) * BLOCK)
            quantise(p_codes[:, cols], p_scales[:, cols], grouped[:])

        def score_block(b):
            cols = slice(b * BLOCK, (b + 1) * BLOCK)
            accs = []
            for t in range(A_TILES):
                acc = new_scores()
                score(t, acc[:], p_codes[:, cols], p_scales[:, cols])
                accs.append(acc)
            return accs

        def score_anchors():
            accs = []
            for t in range(A_TILES):
                acc = new_scores()
                for place in range(A_TILES):
                    other = (t + place) % A_TILES
                    cols = slice(other * P, (other + 1) * P)
                    score(t, acc[:, place * P : (place + 1) * P], a_codes[:, cols], a_scales[:, cols])
                accs.append(acc)
            return accs

        own = keep.tile([P, A_TILES, P], F32)

        def reduce_anchors(t, acc):
            find_largest(OTHER_TILES, slice(t, t + 1), acc[:, P:BLOCK])
            nc.vector.tensor_add(out=own[:, t, :], in0=acc[:, 0:P], in1=mask[:])
            scale_largest(OTHER_TILES, slice(t, t + 1))

        a_grouped = new_grouped()
        a_banks = [transposes(a_raw_words, bank) for bank in range(BANKS)]
        half = N_A // BANKS
        for bank in range(BANKS):
            empty_bank(nc.scalar.copy, a_grouped, bank, a_banks[bank])
            cols = slice(bank * half, (bank + 1) * half)
            quantise(a_codes[:, cols], a_scales[:, cols], a_grouped[:, cols.start * PACK : cols.stop * PACK])
        grouped = {}
        grouped[0] = new_grouped()
        grouped[1] = new_grouped()
        for bank in range(BANKS):
            empty_bank(nc.scalar.copy, grouped[0], bank, transposes(block_words(0), bank))
        anchor_accs = score_anchors()
        for t in range(2):
            reduce_anchors(t, anchor_accs[t])
            exponential(OTHER_TILES, t, anchor_accs[t][:, P:BLOCK])
        quantise_block(0, grouped[0])
        for bank in range(BANKS):
            empty_bank(nc.scalar.copy, grouped[1], bank, transposes(block_words(1), bank))

        for i in range(N_BLOCKS + 1):
            accs = anchor_accs if i == 0 else score_block(i - 1)
            s = FIRST_BLOCK + i - 1
            ahead = i + 2
            if ahead < N_BLOCKS:
                banks = [transposes(block_words(ahead), bank) for bank in range(BANKS)]
                grouped[ahead] = new_grouped()
            for t in range(A_TILES):
                tile_t = slice(t, t + 1)
                if i == 0:
                    if t > 1:
                        reduce_anchors(t, accs[t])
                        exponential(OTHER_TILES, t, accs[t][:, P:BLOCK])
                else:
                    find_largest(s, tile_t, accs[t][:])
                    scale_largest(s, tile_t)
                    exponential(s, t, accs[t][:])
                if t % 2 == 1 and ahead < N_BLOCKS:
                    bank = t // 2
                    on_vector = bank == 1 and i % 2 == 1
                    empty_bank(
                        nc.vector.tensor_copy if on_vector else nc.scalar.copy, grouped[ahead], bank, banks[bank]
                    )
            if i == 0:
                find_largest(OWN_TILE, slice(0, A_TILES), own[:])
                scale_largest(OWN_TILE, slice(0, A_TILES))
                for t in range(A_TILES):
                    exponential(OWN_TILE, t, own[:, t, :])
            if ahead - 1 < N_BLOCKS:
                quantise_block(ahead - 1, grouped[ahead - 1])

        weigh()
        inverse = keep.tile([P, A_TILES], F32)
        nc.vector.reciprocal(out=inverse[:], in_=total[:, :, ALL])
        nc.vector.tensor_mul(out=ratio[:, 0:A_TILES], in0=inverse[:], in1=total[:, :, POSITIVES])

        shift_rows = new_words()
        nc.tensor.transpose(shift_rows[:, 0, 0:P], shift[:], identity[:])
        ratio_rows = new_words()
        nc.tensor.transpose(ratio_rows[:, 0, 0:P], ratio[:], identity[:])
        result_rows = keep.tile([P, P], F32)
        nc.scalar.activation(out=result_rows[:], in_=ratio_rows[:, 0, 0:P], func=ACT.Ln)
        nc.vector.tensor_add(out=result_rows[:], in0=result_rows[:], in1=shift_rows[:, 0, 0:P])
        nc.sync.dma_start(out=out.rearrange("(t p) -> t p", p=P), in_=result_rows[0:A_TILES, :])
